import numpy as np
import ml_dtypes


def mxq(x, axis, fmt="e4m3"):
    dtype, down = {"e4m3": (ml_dtypes.float8_e4m3fn, 7), "e5m2": (ml_dtypes.float8_e5m2, 14)}[fmt]
    v = np.moveaxis(np.asarray(x, np.float32).astype(ml_dtypes.bfloat16).astype(np.float64), axis, -1)
    blocks = v.reshape(v.shape[:-1] + (-1, 32))
    amax = np.abs(blocks).max(-1, keepdims=True)
    byte = np.maximum(np.where(amax > 0, np.frexp(amax)[1] - 1 + 127, 0) - down, 1)
    scale = np.exp2(byte - 127.0)
    codes = (blocks / scale).astype(np.float32).astype(dtype).astype(np.float64)
    return np.moveaxis((codes * scale).reshape(v.shape), -1, axis)


WIDE = False


def mx_kscale(k):
    if not WIDE:
        return np.ones(k)
    levels = np.array([10, -10, 5, -5, 0])
    a = np.random.permutation(np.resize(levels, k // 512 * 4)).reshape(k // 512, 4)
    idx = np.arange(k)
    return np.exp2(a[idx // 512, idx % 128 // 32])


BF16 = ml_dtypes.bfloat16


def bf(x):
    return np.asarray(x, np.float32).astype(BF16)


def f64(x):
    return np.asarray(x).astype(np.float64)


E2M1 = np.array([0.0, 0.5, 1.0, 1.5, 2.0, 3.0, 4.0, 6.0, -0.0, -0.5, -1.0, -1.5, -2.0, -3.0, -4.0, -6.0])


def pack_weight(w, fmt):
    k, n = w.shape
    w = f64(bf(w)).reshape(k // 32, 32, n)
    amax = np.abs(w).max(1)
    if fmt == "e4m3":
        byte = np.frexp(amax)[1] - 1 + 127 - 7
    else:
        mant, ex = np.frexp(amax / 6.0)
        byte = np.where(mant > 0.5, ex, ex - 1) + 127
    byte = np.clip(np.where(amax > 0, byte, 1), 1, 254)
    scaled = (w * np.exp2(127.0 - byte)[:, None, :]).reshape(k, n).astype(np.float32)
    by_word = np.ascontiguousarray(scaled.reshape(k // 512, 128, 4, n).transpose(0, 1, 3, 2))
    if fmt == "e4m3":
        words = by_word.astype(ml_dtypes.float8_e4m3fn).view(np.uint8)
    else:
        c = by_word.astype(ml_dtypes.float4_e2m1fn).view(np.uint8) & 0xF
        words = c[..., 0::2] | (c[..., 1::2] << 4)
    return np.ascontiguousarray(words), np.ascontiguousarray(byte.astype(np.uint8).reshape(k // 512, 16, n))


def unpack_weight(words, scales, fmt):
    g, p, n, _ = words.shape
    if fmt == "e4m3":
        vals = np.ascontiguousarray(words).view(ml_dtypes.float8_e4m3fn).astype(np.float64)
    else:
        nib = np.empty((g, p, n, 4), np.uint8)
        nib[..., 0::2] = words & 0xF
        nib[..., 1::2] = words >> 4
        vals = E2M1[nib]
    vals = vals * np.repeat(np.exp2(scales.astype(np.float64) - 127.0), 8, axis=1)[..., None]
    return vals.transpose(0, 1, 3, 2).reshape(g * 512, n)

def pack4(w):
    words, scales = pack_weight(w, "e2m1")
    return words.reshape(words.shape[0], 128, -1), scales


def unpack4(words, scales):
    return unpack_weight(words.reshape(words.shape[0], 128, -1, 2), scales, "e2m1")


B, CIN, CMID, C4, C8, COUT, T, H, W = 2, 1024, 1024, 256, 128, 128, 4, 16, 16
S = T * H * W


def setup_inputs():
    s = mx_kscale(CMID)
    h_add = np.maximum(np.random.standard_normal((B, CMID, S)) * np.sqrt(2.0), 0.0)
    h_occ = np.maximum(np.random.standard_normal((B, C8, S)) * np.sqrt(2.0), 0.0)
    w_add2 = np.random.standard_normal((CIN, CMID)) * np.sqrt(2.0 / CMID) / s[None, :]
    words, scales = pack4(np.ascontiguousarray(w_add2.T))
    return {"h_add": bf(h_add * s[None, :, None]),
            "w_add2_words": words,
            "w_add2_scales": scales,
            "b_add2": bf(np.random.standard_normal(CIN) * 0.3),
            "h_occ": bf(h_occ),
            "w_occ3": bf(np.random.standard_normal((COUT, C8)) / np.sqrt(C8))}


def reference(h_add, w_add2_words, w_add2_scales, b_add2, h_occ, w_occ3):
    feat = (unpack4(w_add2_words, w_add2_scales).T @ mxq(f64(h_add), 1, "e4m3")) + f64(b_add2)[None, :, None]
    occ = np.abs(f64(w_occ3) @ f64(h_occ))
    return (mxq(occ, 2, "e4m3") @ mxq(feat, 2, "e4m3").transpose(0, 2, 1)) / S

@@ -1,0 +1,205 @@
+from contextlib import ExitStack
+
+import concourse.masks as masks
+import concourse.mybir as mybir
+
+F32 = mybir.dt.float32
+BF16 = mybir.dt.bfloat16
+I32 = mybir.dt.int32
+U32 = mybir.dt.uint32
+U8 = mybir.dt.uint8
+FP8X4 = mybir.dt.float8_e4m3fn_x4
+FP4X4 = mybir.dt.float4_e2m1fn_x4
+ACT = mybir.ActivationFunctionType
+ALU = mybir.AluOpType
+
+P = 128
+PACK = 4
+K_PASS = P * PACK
+BANK = 512
+
+B = 2
+CMID = 1024
+CIN = 1024
+C8 = 128
+COUT = 128
+S = 1024
+
+K_PASSES = CMID // K_PASS
+V_PASSES = S // K_PASS
+N_CHUNKS = B * V_PASSES
+HALVES = CIN // BANK
+BANKS_PER_HALF = BANK // P
+
+FLOPS = 2 * B * S * (CIN * CMID + COUT * C8 + COUT * CIN)
+
+
+def tile_occurrencepool_pa_kernel(
+    tc, h_add, w_add2_words, w_add2_scales, b_add2, h_occ, w_occ3, out
+):
+    nc = tc.nc
+    with ExitStack() as ctx:
+        consts = ctx.enter_context(tc.tile_pool(name="consts", bufs=1))
+        raws = ctx.enter_context(tc.tile_pool(name="raws", bufs=N_CHUNKS))
+        work = ctx.enter_context(tc.tile_pool(name="work", bufs=3))
+        psum_head = ctx.enter_context(tc.psum_pool(name="psum_head", bufs=2))
+        psum_feat = ctx.enter_context(tc.psum_pool(name="psum_feat", bufs=4))
+        psum_acc = ctx.enter_context(tc.psum_pool(name="psum_acc", bufs=HALVES))
+
+        w_scales = consts.tile([P, K_PASSES, CIN], U8, align_bytes=64)
+        nc.vector.memset(w_scales[:].bitcast(I32), 0)
+
+        def load_h(i):
+            b, vg = divmod(i, V_PASSES)
+            raw = raws.tile([P, K_PASSES, PACK, K_PASS], BF16, name="h_raw")
+            for g in range(K_PASSES):
+                nc.sync.dma_start(
+                    out=raw[:, g],
+                    in_=h_add[
+                        b, g * K_PASS : (g + 1) * K_PASS, vg * K_PASS : (vg + 1) * K_PASS
+                    ].rearrange("(p t) v -> p t v", t=PACK),
+                )
+            return raw
+
+        h_raw = [load_h(0)]
+        for quadrant in range(4):
+            nc.sync.dma_start(
+                out=w_scales[32 * quadrant : 32 * quadrant + 4].bitcast(I32),
+                in_=w_add2_scales[:, 4 * quadrant : 4 * quadrant + 4, :]
+                .rearrange("g r n -> r g n")
+                .bitcast(I32),
+            )
+        w_words = consts.tile([P, K_PASSES, 2 * CIN], U8, align_bytes=64)
+        nc.sync.dma_start(
+            out=w_words[:].bitcast(I32),
+            in_=w_add2_words.rearrange("g p n -> p g n").bitcast(I32),
+        )
+        h_raw.append(load_h(1))
+        h_occ_sb = consts.tile([C8, B, S], BF16)
+        nc.sync.dma_start(out=h_occ_sb[:], in_=h_occ.rearrange("b c v -> c b v"))
+        h_raw.append(load_h(2))
+        h_raw.append(load_h(3))
+
+        w_occ_sb = consts.tile([COUT, C8], BF16)
+        nc.scalar.dma_start(out=w_occ_sb[:], in_=w_occ3)
+        bias_row = consts.tile([P, CIN], BF16)
+        nc.gpsimd.memset(bias_row[:], 0.0)
+        nc.scalar.dma_start(out=bias_row[0:1, :], in_=b_add2.rearrange("(o c) -> o c", o=1))
+
+        ones = consts.tile([P, P], BF16)
+        nc.gpsimd.memset(ones[:], 1.0)
+        bias_all = consts.tile([P, CIN], F32)
+        for half in range(HALVES):
+            cols = slice(half * BANK, (half + 1) * BANK)
+            bias_ps = psum_head.tile([P, BANK], F32, tag="head")
+            nc.tensor.matmul(bias_ps[:], lhsT=ones[:], rhs=bias_row[:, cols], start=True, stop=True)
+            nc.scalar.copy(out=bias_all[:, cols], in_=bias_ps[:])
+
+        identity = consts.tile([P, P], BF16)
+        masks.make_identity(nc, identity[:])
+        w_occT_ps = psum_head.tile([C8, COUT], BF16, tag="head")
+        nc.tensor.transpose(w_occT_ps[:], w_occ_sb[:], identity[:])
+        w_occT = consts.tile([C8, COUT], BF16)
+        nc.scalar.copy(out=w_occT[:], in_=w_occT_ps[:])
+
+        occ_grp = consts.tile([P, N_CHUNKS, COUT, PACK], BF16, align_bytes=64)
+        for i in range(N_CHUNKS):
+            b, vg = divmod(i, V_PASSES)
+            occ_ps = psum_head.tile([P, PACK, COUT], F32, tag="head")
+            for t in range(PACK):
+                v0 = vg * K_PASS + t * P
+                nc.tensor.matmul(
+                    occ_ps[:, t, :],
+                    lhsT=h_occ_sb[:, b, v0 : v0 + P],
+                    rhs=w_occT[:],
+                    start=True,
+                    stop=True,
+                )
+            nc.scalar.activation(
+                out=occ_grp[:, i], in_=occ_ps[:].rearrange("p t o -> p o t"), func=ACT.Abs
+            )
+        occ_codes = consts.tile([P, N_CHUNKS, COUT], U32, align_bytes=64)
+        occ_scales = consts.tile([P, N_CHUNKS, COUT], U8, align_bytes=64)
+        nc.vector.quantize_mx(
+            out=occ_codes[:].rearrange("p i o -> p (i o)").bitcast(FP8X4),
+            scales=occ_scales[:].rearrange("p i o -> p (i o)"),
+            in_=occ_grp[:].rearrange("p i o t -> p (i o t)"),
+        )
+
+        def regroup_h(i):
+            copy = nc.vector.tensor_copy if i == 0 else nc.scalar.copy
+            grp = work.tile([P, K_PASSES, K_PASS, PACK], BF16, name="h_grp", align_bytes=64)
+            for g in range(K_PASSES):
+                copy(out=grp[:, g], in_=h_raw[i][:, g].rearrange("p t v -> p v t"))
+            return grp
+
+        def quantise_h(grp):
+            codes = work.tile([P, K_PASSES, K_PASS], U32, name="h_codes", align_bytes=64)
+            scales = work.tile([P, K_PASSES, K_PASS], U8, name="h_scales", align_bytes=64)
+            nc.vector.quantize_mx(
+                out=codes[:].rearrange("p g v -> p (g v)").bitcast(FP8X4),
+                scales=scales[:].rearrange("p g v -> p (g v)"),
+                in_=grp[:].rearrange("p g v t -> p (g v t)"),
+            )
+            return codes, scales
+
+        def feature_bank(h_codes, h_scales, c0, f_grp_cols):
+            feat_ps = psum_feat.tile([P, PACK, P], F32, name="feat_ps")
+            for t in range(PACK):
+                voxels = slice(t * P, (t + 1) * P)
+                for g in range(K_PASSES):
+                    nc.tensor.matmul_mx(
+                        out=feat_ps[:, t, :],
+                        lhsT=h_codes[:, g, voxels].bitcast(FP8X4),
+                        lhsT_scale=h_scales[:, g, voxels],
+                        rhs=w_words[:, g, 2 * c0 : 2 * (c0 + P)].bitcast(FP4X4),
+                        rhs_scale=w_scales[:, g, c0 : c0 + P],
+                        start=(g == 0),
+                        stop=(g == K_PASSES - 1),
+                    )
+            nc.vector.tensor_tensor(
+                out=f_grp_cols,
+                in0=feat_ps[:].rearrange("p t c -> p c t"),
+                in1=bias_all[:, c0 : c0 + P].unsqueeze(2).to_broadcast([P, P, PACK]),
+                op=ALU.add,
+            )
+
+        h_next = quantise_h(regroup_h(0))
+        acc = []
+        for i in range(N_CHUNKS):
+            b, vg = divmod(i, V_PASSES)
+            h_codes, h_scales = h_next
+            if i + 1 < N_CHUNKS:
+                grp_next = regroup_h(i + 1)
+            if vg == 0:
+                acc = [psum_acc.tile([COUT, BANK], F32, name="acc") for half in range(HALVES)]
+            for half in range(HALVES):
+                f_grp = work.tile([P, BANK, PACK], BF16, name="f_grp", align_bytes=64)
+                for j in range(BANKS_PER_HALF):
+                    feature_bank(
+                        h_codes, h_scales, half * BANK + j * P, f_grp[:, j * P : (j + 1) * P, :]
+                    )
+                if half == 0 and i + 1 < N_CHUNKS:
+                    h_next = quantise_h(grp_next)
+                f_codes = work.tile([P, BANK], U32, name="f_codes", align_bytes=64)
+                f_scales = work.tile([P, BANK], U8, name="f_scales", align_bytes=64)
+                nc.vector.quantize_mx(
+                    out=f_codes[:].bitcast(FP8X4),
+                    scales=f_scales[:],
+                    in_=f_grp[:].rearrange("p c t -> p (c t)"),
+                )
+                nc.tensor.matmul_mx(
+                    out=acc[half][:],
+                    lhsT=occ_codes[:, i, :].bitcast(FP8X4),
+                    lhsT_scale=occ_scales[:, i, :],
+                    rhs=f_codes[:].bitcast(FP8X4),
+                    rhs_scale=f_scales[:],
+                    start=(vg == 0),
+                    stop=(vg == V_PASSES - 1),
+                )
+                if vg == V_PASSES - 1:
+                    out_sb = work.tile([COUT, BANK], F32, name="out_sb")
+                    nc.scalar.activation(out=out_sb[:], in_=acc[half][:], func=ACT.Copy, scale=1.0 / S)
+                    nc.sync.dma_start(
+                        out=out[b, :, half * BANK : (half + 1) * BANK], in_=out_sb[:]
+                    )

@@ -31,6 +31,12 @@ N_CHUNKS = B * V_PASSES
 HALVES = CIN // BANK
 BANKS_PER_HALF = BANK // P
 
+WORDS = PACK // 2
+TILES = CIN // P
+PIECE = K_PASS // 2
+PIECES = K_PASSES * 2
+TURNED = (0, BANKS_PER_HALF)
+
 FLOPS = 2 * B * S * (CIN * CMID + COUT * C8 + COUT * CIN)
 
 
@@ -41,13 +47,11 @@ def tile_occurrencepool_pa_kernel(
     with ExitStack() as ctx:
         consts = ctx.enter_context(tc.tile_pool(name="consts", bufs=1))
         raws = ctx.enter_context(tc.tile_pool(name="raws", bufs=N_CHUNKS))
-        work = ctx.enter_context(tc.tile_pool(name="work", bufs=3))
-        psum_head = ctx.enter_context(tc.psum_pool(name="psum_head", bufs=2))
+        work = ctx.enter_context(tc.tile_pool(name="work", bufs=4))
         psum_feat = ctx.enter_context(tc.psum_pool(name="psum_feat", bufs=4))
-        psum_acc = ctx.enter_context(tc.psum_pool(name="psum_acc", bufs=HALVES))
-
-        w_scales = consts.tile([P, K_PASSES, CIN], U8, align_bytes=64)
-        nc.vector.memset(w_scales[:].bitcast(I32), 0)
+        psum_chan = ctx.enter_context(tc.psum_pool(name="psum_chan", bufs=2))
+        psum_misc = ctx.enter_context(tc.psum_pool(name="psum_misc", bufs=2))
+        ctx.enter_context(tc.manual_schedule())
 
         def load_h(i):
             b, vg = divmod(i, V_PASSES)
@@ -61,7 +65,22 @@ def tile_occurrencepool_pa_kernel(
                 )
             return raw
 
+        ones = consts.tile([P, P], BF16)
+        nc.vector.memset(ones[:], 1.0)
+        warm = consts.tile([P, 1], F32)
+        nc.scalar.activation(out=warm[:], in_=ones[:, 0:1], func=ACT.Abs)
+
+        w_scales = consts.tile([P, K_PASSES, CIN], U8, align_bytes=64)
+        nc.vector.memset(w_scales[:].bitcast(I32), 0)
+        bias_row = consts.tile([P, CIN], BF16)
+        nc.gpsimd.memset(bias_row[:], 0.0)
+        identity = consts.tile([P, P], BF16)
+        masks.make_identity(nc, identity[:])
+        identity_f32 = consts.tile([P, P], F32)
+        masks.make_identity(nc, identity_f32[:])
+
         h_raw = [load_h(0)]
+        nc.sync.dma_start(out=bias_row[0:1, :], in_=b_add2.rearrange("(o c) -> o c", o=1))
         for quadrant in range(4):
             nc.sync.dma_start(
                 out=w_scales[32 * quadrant : 32 * quadrant + 4].bitcast(I32),
@@ -70,42 +89,148 @@ def tile_occurrencepool_pa_kernel(
                 .bitcast(I32),
             )
         w_words = consts.tile([P, K_PASSES, 2 * CIN], U8, align_bytes=64)
-        nc.sync.dma_start(
-            out=w_words[:].bitcast(I32),
-            in_=w_add2_words.rearrange("g p n -> p g n").bitcast(I32),
-        )
+        for half in range(HALVES):
+            cols = slice(half * 2 * BANK, (half + 1) * 2 * BANK)
+            nc.sync.dma_start(
+                out=w_words[:, :, cols].bitcast(I32),
+                in_=w_add2_words[:, :, cols].rearrange("g p n -> p g n").bitcast(I32),
+            )
         h_raw.append(load_h(1))
+        w_occ_sb = consts.tile([COUT, C8], BF16)
+        nc.sync.dma_start(out=w_occ_sb[:], in_=w_occ3)
         h_occ_sb = consts.tile([C8, B, S], BF16)
         nc.sync.dma_start(out=h_occ_sb[:], in_=h_occ.rearrange("b c v -> c b v"))
         h_raw.append(load_h(2))
         h_raw.append(load_h(3))
 
-        w_occ_sb = consts.tile([COUT, C8], BF16)
-        nc.scalar.dma_start(out=w_occ_sb[:], in_=w_occ3)
-        bias_row = consts.tile([P, CIN], BF16)
-        nc.gpsimd.memset(bias_row[:], 0.0)
-        nc.scalar.dma_start(out=bias_row[0:1, :], in_=b_add2.rearrange("(o c) -> o c", o=1))
+        h_grp = []
+        h_codes = []
+        h_scales = []
+        for i in range(N_CHUNKS):
+            grp = work.tile([P, K_PASSES, K_PASS, PACK], BF16, name="h_grp", align_bytes=64)
+            codes = work.tile([P, K_PASSES, K_PASS], U32, name="h_codes", align_bytes=64)
+            scales = work.tile([P, K_PASSES, K_PASS], U8, name="h_scales", align_bytes=64)
+            h_grp.append(grp)
+            h_codes.append(codes)
+            h_scales.append(scales)
 
-        ones = consts.tile([P, P], BF16)
-        nc.gpsimd.memset(ones[:], 1.0)
-        bias_all = consts.tile([P, CIN], F32)
-        for half in range(HALVES):
-            cols = slice(half * BANK, (half + 1) * BANK)
-            bias_ps = psum_head.tile([P, BANK], F32, tag="head")
-            nc.tensor.matmul(bias_ps[:], lhsT=ones[:], rhs=bias_row[:, cols], start=True, stop=True)
-            nc.scalar.copy(out=bias_all[:, cols], in_=bias_ps[:])
+        def regroup(i, g, v0, v1, engine):
+            dst = h_grp[i][:, g, v0:v1, :]
+            src = h_raw[i][:, g, :, v0:v1].rearrange("p t v -> p v t")
+            if engine == "vector":
+                nc.vector.tensor_copy(out=dst, in_=src)
+            elif engine == "gpsimd":
+                nc.gpsimd.tensor_scalar(
+                    out=dst, in0=src, scalar1=1.0, scalar2=0.0, op0=ALU.mult, op1=ALU.add
+                )
+            else:
+                nc.scalar.copy(out=dst, in_=src)
 
-        identity = consts.tile([P, P], BF16)
-        masks.make_identity(nc, identity[:])
-        w_occT_ps = psum_head.tile([C8, COUT], BF16, tag="head")
-        nc.tensor.transpose(w_occT_ps[:], w_occ_sb[:], identity[:])
-        w_occT = consts.tile([C8, COUT], BF16)
-        nc.scalar.copy(out=w_occT[:], in_=w_occT_ps[:])
+        def regroup_piece(r):
+            i, q = divmod(r, PIECES)
+            if i < N_CHUNKS:
+                g, part = divmod(q, 2)
+                regroup(
+                    i, g, part * PIECE, (part + 1) * PIECE, "gpsimd" if q == PIECES - 1 else "scalar"
+                )
+
+        def quantise_h(i, g):
+            if i < N_CHUNKS:
+                nc.vector.quantize_mx(
+                    out=h_codes[i][:, g].bitcast(FP8X4),
+                    scales=h_scales[i][:, g],
+                    in_=h_grp[i][:, g].rearrange("p v t -> p (v t)"),
+                )
+
+        f_grp = {}
+        f_codes = {}
+        f_scales = {}
+
+        def open_half(i, half):
+            grp = work.tile([P, BANK, PACK], BF16, name="f_grp", align_bytes=64)
+            codes = work.tile([P, BANK], U32, name="f_codes", align_bytes=64)
+            scales = work.tile([P, BANK], U8, name="f_scales", align_bytes=64)
+            f_grp[i, half] = grp
+            f_codes[i, half] = codes
+            f_scales[i, half] = scales
+
+        def tile_cols(i, tile):
+            half, j = divmod(tile, BANKS_PER_HALF)
+            return f_grp[i, half][:, j * P : (j + 1) * P, :]
+
+        def feature_bank(i, tile):
+            c0 = tile * P
+            feat_ps = psum_feat.tile([P, PACK, P], F32, name="feat_ps")
+            for t in range(PACK):
+                voxels = slice(t * P, (t + 1) * P)
+                for g in range(K_PASSES):
+                    nc.tensor.matmul_mx(
+                        out=feat_ps[:, t, :],
+                        lhsT=h_codes[i][:, g, voxels].bitcast(FP8X4),
+                        lhsT_scale=h_scales[i][:, g, voxels],
+                        rhs=w_words[:, g, 2 * c0 : 2 * (c0 + P)].bitcast(FP4X4),
+                        rhs_scale=w_scales[:, g, c0 : c0 + P],
+                        start=(g == 0),
+                        stop=(g == K_PASSES - 1),
+                    )
+            nc.vector.tensor_tensor(
+                out=tile_cols(i, tile),
+                in0=feat_ps[:].rearrange("p t c -> p c t"),
+                in1=bias_all[:, c0 : c0 + P].unsqueeze(2).to_broadcast([P, P, PACK]),
+                op=ALU.add,
+            )
+
+        def turned_bank(i, tile):
+            c0 = tile * P
+            chan_ps = psum_chan.tile([P, K_PASS], F32, name="chan_ps")
+            for g in range(K_PASSES):
+                nc.tensor.matmul_mx(
+                    out=chan_ps[:],
+                    lhsT=w_words[:, g, 2 * c0 : 2 * (c0 + P)].bitcast(FP4X4),
+                    lhsT_scale=w_scales[:, g, c0 : c0 + P],
+                    rhs=h_codes[i][:, g, :].bitcast(FP8X4),
+                    rhs_scale=h_scales[i][:, g, :],
+                    start=(g == 0),
+                    stop=(g == K_PASSES - 1),
+                )
+            chan = work.tile([P, WORDS, P, 2], BF16, name="chan", align_bytes=64)
+            k = TURNED.index(tile)
+            nc.scalar.activation(
+                out=chan[:],
+                in_=chan_ps[:].rearrange("c (u e p) -> c u p e", u=WORDS, e=2),
+                func=ACT.Identity,
+                bias=turned_bias[:, k : k + 1],
+            )
+            return chan
+
+        def turn(i, chans):
+            turned_ps = psum_misc.tile([P, len(TURNED), WORDS, P], F32, tag="misc")
+            for k, chan in enumerate(chans):
+                words = chan[:].rearrange("c u p e -> c (u p e)").bitcast(F32)
+                for u in range(WORDS):
+                    nc.tensor.transpose(
+                        turned_ps[:, k, u, :], words[:, u * P : (u + 1) * P], identity_f32[:]
+                    )
+            for k, tile in enumerate(TURNED):
+                nc.scalar.copy(
+                    out=tile_cols(i, tile).rearrange("p c t -> p (c t)").bitcast(F32),
+                    in_=turned_ps[:, k].rearrange("p u c -> p c u"),
+                )
+
+        def quantise_f(i, half, c0, c1):
+            nc.vector.quantize_mx(
+                out=f_codes[i, half][:, c0:c1].bitcast(FP8X4),
+                scales=f_scales[i, half][:, c0:c1],
+                in_=f_grp[i, half][:, c0:c1].rearrange("p c t -> p (c t)"),
+            )
 
         occ_grp = consts.tile([P, N_CHUNKS, COUT, PACK], BF16, align_bytes=64)
-        for i in range(N_CHUNKS):
+        occ_codes = consts.tile([P, N_CHUNKS, COUT], U32, align_bytes=64)
+        occ_scales = consts.tile([P, N_CHUNKS, COUT], U8, align_bytes=64)
+
+        def occurrence(i):
             b, vg = divmod(i, V_PASSES)
-            occ_ps = psum_head.tile([P, PACK, COUT], F32, tag="head")
+            occ_ps = psum_misc.tile([P, PACK, COUT], F32, tag="misc")
             for t in range(PACK):
                 v0 = vg * K_PASS + t * P
                 nc.tensor.matmul(
@@ -118,88 +243,125 @@ def tile_occurrencepool_pa_kernel(
             nc.scalar.activation(
                 out=occ_grp[:, i], in_=occ_ps[:].rearrange("p t o -> p o t"), func=ACT.Abs
             )
-        occ_codes = consts.tile([P, N_CHUNKS, COUT], U32, align_bytes=64)
-        occ_scales = consts.tile([P, N_CHUNKS, COUT], U8, align_bytes=64)
-        nc.vector.quantize_mx(
-            out=occ_codes[:].rearrange("p i o -> p (i o)").bitcast(FP8X4),
-            scales=occ_scales[:].rearrange("p i o -> p (i o)"),
-            in_=occ_grp[:].rearrange("p i o t -> p (i o t)"),
-        )
 
-        def regroup_h(i):
-            copy = nc.vector.tensor_copy if i == 0 else nc.scalar.copy
-            grp = work.tile([P, K_PASSES, K_PASS, PACK], BF16, name="h_grp", align_bytes=64)
-            for g in range(K_PASSES):
-                copy(out=grp[:, g], in_=h_raw[i][:, g].rearrange("p t v -> p v t"))
-            return grp
-
-        def quantise_h(grp):
-            codes = work.tile([P, K_PASSES, K_PASS], U32, name="h_codes", align_bytes=64)
-            scales = work.tile([P, K_PASSES, K_PASS], U8, name="h_scales", align_bytes=64)
+        def quantise_occ(b):
+            sample = slice(b * V_PASSES, (b + 1) * V_PASSES)
             nc.vector.quantize_mx(
-                out=codes[:].rearrange("p g v -> p (g v)").bitcast(FP8X4),
-                scales=scales[:].rearrange("p g v -> p (g v)"),
-                in_=grp[:].rearrange("p g v t -> p (g v t)"),
-            )
-            return codes, scales
-
-        def feature_bank(h_codes, h_scales, c0, f_grp_cols):
-            feat_ps = psum_feat.tile([P, PACK, P], F32, name="feat_ps")
-            for t in range(PACK):
-                voxels = slice(t * P, (t + 1) * P)
-                for g in range(K_PASSES):
-                    nc.tensor.matmul_mx(
-                        out=feat_ps[:, t, :],
-                        lhsT=h_codes[:, g, voxels].bitcast(FP8X4),
-                        lhsT_scale=h_scales[:, g, voxels],
-                        rhs=w_words[:, g, 2 * c0 : 2 * (c0 + P)].bitcast(FP4X4),
-                        rhs_scale=w_scales[:, g, c0 : c0 + P],
-                        start=(g == 0),
-                        stop=(g == K_PASSES - 1),
-                    )
-            nc.vector.tensor_tensor(
-                out=f_grp_cols,
-                in0=feat_ps[:].rearrange("p t c -> p c t"),
-                in1=bias_all[:, c0 : c0 + P].unsqueeze(2).to_broadcast([P, P, PACK]),
-                op=ALU.add,
+                out=occ_codes[:, sample].rearrange("p i o -> p (i o)").bitcast(FP8X4),
+                scales=occ_scales[:, sample].rearrange("p i o -> p (i o)"),
+                in_=occ_grp[:, sample].rearrange("p i o t -> p (i o t)"),
             )
 
-        h_next = quantise_h(regroup_h(0))
-        acc = []
-        for i in range(N_CHUNKS):
-            b, vg = divmod(i, V_PASSES)
-            h_codes, h_scales = h_next
-            if i + 1 < N_CHUNKS:
-                grp_next = regroup_h(i + 1)
-            if vg == 0:
-                acc = [psum_acc.tile([COUT, BANK], F32, name="acc") for half in range(HALVES)]
-            for half in range(HALVES):
-                f_grp = work.tile([P, BANK, PACK], BF16, name="f_grp", align_bytes=64)
-                for j in range(BANKS_PER_HALF):
-                    feature_bank(
-                        h_codes, h_scales, half * BANK + j * P, f_grp[:, j * P : (j + 1) * P, :]
-                    )
-                if half == 0 and i + 1 < N_CHUNKS:
-                    h_next = quantise_h(grp_next)
-                f_codes = work.tile([P, BANK], U32, name="f_codes", align_bytes=64)
-                f_scales = work.tile([P, BANK], U8, name="f_scales", align_bytes=64)
-                nc.vector.quantize_mx(
-                    out=f_codes[:].bitcast(FP8X4),
-                    scales=f_scales[:],
-                    in_=f_grp[:].rearrange("p c t -> p (c t)"),
-                )
+        def pool_half(b, half, c0, c1, engine):
+            acc = psum_misc.tile([COUT, BANK], F32, tag="misc")
+            for vg in range(V_PASSES):
+                i = b * V_PASSES + vg
                 nc.tensor.matmul_mx(
-                    out=acc[half][:],
+                    out=acc[:, : c1 - c0],
                     lhsT=occ_codes[:, i, :].bitcast(FP8X4),
                     lhsT_scale=occ_scales[:, i, :],
-                    rhs=f_codes[:].bitcast(FP8X4),
-                    rhs_scale=f_scales[:],
+                    rhs=f_codes[i, half][:, c0:c1].bitcast(FP8X4),
+                    rhs_scale=f_scales[i, half][:, c0:c1],
                     start=(vg == 0),
                     stop=(vg == V_PASSES - 1),
                 )
-                if vg == V_PASSES - 1:
-                    out_sb = work.tile([COUT, BANK], F32, name="out_sb")
-                    nc.scalar.activation(out=out_sb[:], in_=acc[half][:], func=ACT.Copy, scale=1.0 / S)
-                    nc.sync.dma_start(
-                        out=out[b, :, half * BANK : (half + 1) * BANK], in_=out_sb[:]
-                    )
+            out_sb = work.tile([COUT, BANK], F32, name="out_sb")
+            if engine == "vector":
+                nc.vector.tensor_scalar(
+                    out=out_sb[:, : c1 - c0],
+                    in0=acc[:, : c1 - c0],
+                    scalar1=1.0 / S,
+                    scalar2=None,
+                    op0=ALU.mult,
+                )
+            else:
+                nc.scalar.activation(
+                    out=out_sb[:, : c1 - c0], in_=acc[:, : c1 - c0], func=ACT.Copy, scale=1.0 / S
+                )
+            nc.sync.dma_start(
+                out=out[b, :, half * BANK + c0 : half * BANK + c1], in_=out_sb[:, : c1 - c0]
+            )
+
+        bias_all = consts.tile([P, CIN], F32)
+        turned_bias = consts.tile([P, len(TURNED)], F32)
+        for g in range(K_PASSES):
+            share = 3 * P
+            regroup(0, g, 0, share, "vector")
+            regroup(0, g, share, K_PASS, "scalar")
+            quantise_h(0, g)
+            cols = slice(g * BANK, (g + 1) * BANK)
+            bias_ps = psum_misc.tile([P, BANK], F32, tag="misc")
+            nc.tensor.matmul(bias_ps[:], lhsT=ones[:], rhs=bias_row[:, cols], start=True, stop=True)
+            nc.scalar.copy(out=bias_all[:, cols], in_=bias_ps[:])
+
+        def head_extras():
+            turned_bias_ps = psum_misc.tile([P, len(TURNED)], F32, tag="misc")
+            for k, tile in enumerate(TURNED):
+                nc.tensor.matmul(
+                    turned_bias_ps[:, k : k + 1],
+                    lhsT=bias_row[:, tile * P : (tile + 1) * P],
+                    rhs=ones[:, 0:1],
+                    start=True,
+                    stop=True,
+                )
+            nc.scalar.copy(out=turned_bias[:], in_=turned_bias_ps[:])
+            w_occT_ps = psum_misc.tile([C8, COUT], BF16, tag="misc")
+            nc.tensor.transpose(w_occT_ps[:], w_occ_sb[:], identity[:])
+            nc.scalar.copy(out=w_occT[:], in_=w_occT_ps[:])
+
+        w_occT = consts.tile([C8, COUT], BF16)
+
+        for i in range(N_CHUNKS):
+            b, vg = divmod(i, V_PASSES)
+            for half in range(HALVES):
+                open_half(i, half)
+            if i == 0:
+                for tile in range(TILES):
+                    feature_bank(i, tile)
+                    if tile < PIECES:
+                        regroup_piece(PIECES + tile)
+                    if tile == 4:
+                        head_extras()
+                        quantise_f(i, 0, 0, BANK)
+                    if tile == 5:
+                        occurrence(0)
+                        occurrence(1)
+                        quantise_h(1, 0)
+                    if tile == 6:
+                        quantise_h(1, 1)
+                        regroup_piece(2 * PIECES)
+                continue
+            chans = [turned_bank(i, TURNED[0])]
+            regroup_piece((i + 1) * PIECES + 1)
+            regroup_piece((i + 1) * PIECES + 3)
+            feature_bank(i, 1)
+            quantise_f(i - 1, 1, 0, BANK)
+            chans.append(turned_bank(i, TURNED[1]))
+            regroup_piece((i + 1) * PIECES + 2)
+            feature_bank(i, 2)
+            if i == 1:
+                quantise_occ(0)
+            if i == 2:
+                quantise_occ(1)
+            quantise_h(i + 1, 0)
+            feature_bank(i, 3)
+            quantise_h(i + 1, 1)
+            turn(i, chans)
+            feature_bank(i, 5)
+            if i == 2:
+                pool_half(0, 1, 0, BANK, "scalar")
+            quantise_f(i, 0, 0, BANK)
+            feature_bank(i, 6)
+            regroup_piece((i + 2) * PIECES)
+            if i == 1:
+                occurrence(2)
+                occurrence(3)
+            if i == N_CHUNKS - 1:
+                quantise_f(i, 1, 0, 2 * P)
+            feature_bank(i, 7)
+            if vg == V_PASSES - 1:
+                pool_half(b, 0, 0, BANK, "scalar")
+        i = N_CHUNKS - 1
+        pool_half(B - 1, 1, 0, 2 * P, "scalar")
+        quantise_f(i, 1, 2 * P, BANK)
+        pool_half(B - 1, 1, 2 * P, BANK, "vector")

@@ -69,6 +69,15 @@ def tile_occurrencepool_pa_kernel(
         nc.vector.memset(ones[:], 1.0)
         warm = consts.tile([P, 1], F32)
         nc.scalar.activation(out=warm[:], in_=ones[:, 0:1], func=ACT.Abs)
+        busy = consts.tile([P, BANK], BF16)
+        nc.vector.memset(busy[:].bitcast(I32), 0)
+
+        def keep_busy(rhs, count):
+            idle_ps = psum_misc.tile([P, BANK], F32, tag="misc")
+            for k in range(count):
+                nc.tensor.matmul(idle_ps[:], lhsT=ones[:], rhs=rhs, start=True, stop=True)
+
+        keep_busy(busy[:], 6)
 
         w_scales = consts.tile([P, K_PASSES, CIN], U8, align_bytes=64)
         nc.vector.memset(w_scales[:].bitcast(I32), 0)
@@ -289,6 +298,7 @@ def tile_occurrencepool_pa_kernel(
             regroup(0, g, 0, share, "vector")
             regroup(0, g, share, K_PASS, "scalar")
             quantise_h(0, g)
+            keep_busy(h_grp[0][:, g, 0:P, :].rearrange("p v t -> p (v t)"), 3)
             cols = slice(g * BANK, (g + 1) * BANK)
             bias_ps = psum_misc.tile([P, BANK], F32, tag="misc")
             nc.tensor.matmul(bias_ps[:], lhsT=ones[:], rhs=bias_row[:, cols], start=True, stop=True)

@@ -128,10 +128,6 @@ def tile_occurrencepool_pa_kernel(
             src = h_raw[i][:, g, :, v0:v1].rearrange("p t v -> p v t")
             if engine == "vector":
                 nc.vector.tensor_copy(out=dst, in_=src)
-            elif engine == "gpsimd":
-                nc.gpsimd.tensor_scalar(
-                    out=dst, in0=src, scalar1=1.0, scalar2=0.0, op0=ALU.mult, op1=ALU.add
-                )
             else:
                 nc.scalar.copy(out=dst, in_=src)
 
@@ -140,7 +136,7 @@ def tile_occurrencepool_pa_kernel(
             if i < N_CHUNKS:
                 g, part = divmod(q, 2)
                 regroup(
-                    i, g, part * PIECE, (part + 1) * PIECE, "gpsimd" if q == PIECES - 1 else "scalar"
+                    i, g, part * PIECE, (part + 1) * PIECE, "vector" if q == 0 else "scalar"
                 )
 
         def quantise_h(i, g):
@@ -343,7 +339,6 @@ def tile_occurrencepool_pa_kernel(
                 continue
             chans = [turned_bank(i, TURNED[0])]
             regroup_piece((i + 1) * PIECES + 1)
-            regroup_piece((i + 1) * PIECES + 3)
             feature_bank(i, 1)
             quantise_f(i - 1, 1, 0, BANK)
             chans.append(turned_bank(i, TURNED[1]))
@@ -355,9 +350,10 @@ def tile_occurrencepool_pa_kernel(
                 quantise_occ(1)
             quantise_h(i + 1, 0)
             feature_bank(i, 3)
-            quantise_h(i + 1, 1)
             turn(i, chans)
+            regroup_piece((i + 1) * PIECES + 3)
             feature_bank(i, 5)
+            quantise_h(i + 1, 1)
             if i == 2:
                 pool_half(0, 1, 0, BANK, "scalar")
             quantise_f(i, 0, 0, BANK)

@@ -51,7 +51,6 @@ def tile_occurrencepool_pa_kernel(
         psum_feat = ctx.enter_context(tc.psum_pool(name="psum_feat", bufs=4))
         psum_chan = ctx.enter_context(tc.psum_pool(name="psum_chan", bufs=2))
         psum_misc = ctx.enter_context(tc.psum_pool(name="psum_misc", bufs=2))
-        ctx.enter_context(tc.manual_schedule())
 
         def load_h(i):
             b, vg = divmod(i, V_PASSES)
@@ -65,31 +64,21 @@ def tile_occurrencepool_pa_kernel(
                 )
             return raw
 
-        ones = consts.tile([P, P], BF16)
-        nc.vector.memset(ones[:], 1.0)
-        warm = consts.tile([P, 1], F32)
-        nc.scalar.activation(out=warm[:], in_=ones[:, 0:1], func=ACT.Abs)
-        busy = consts.tile([P, BANK], BF16)
-        nc.vector.memset(busy[:].bitcast(I32), 0)
-
-        def keep_busy(rhs, count):
-            idle_ps = psum_misc.tile([P, BANK], F32, tag="misc")
-            for k in range(count):
-                nc.tensor.matmul(idle_ps[:], lhsT=ones[:], rhs=rhs, start=True, stop=True)
-
-        keep_busy(busy[:], 6)
-
+        bias_row = consts.tile([P, CIN], BF16)
+        nc.vector.memset(bias_row[:].bitcast(I32), 0)
+        nc.scalar.dma_start(out=bias_row[0:1, :], in_=b_add2.rearrange("(o c) -> o c", o=1))
         w_scales = consts.tile([P, K_PASSES, CIN], U8, align_bytes=64)
         nc.vector.memset(w_scales[:].bitcast(I32), 0)
-        bias_row = consts.tile([P, CIN], BF16)
-        nc.gpsimd.memset(bias_row[:], 0.0)
+        ones = consts.tile([P, P], BF16)
+        nc.gpsimd.memset(ones[:], 1.0)
+        warm = consts.tile([P, 1], F32)
+        nc.scalar.activation(out=warm[:], in_=ones[:, 0:1], func=ACT.Abs)
         identity = consts.tile([P, P], BF16)
         masks.make_identity(nc, identity[:])
         identity_f32 = consts.tile([P, P], F32)
         masks.make_identity(nc, identity_f32[:])
 
         h_raw = [load_h(0)]
-        nc.sync.dma_start(out=bias_row[0:1, :], in_=b_add2.rearrange("(o c) -> o c", o=1))
         for quadrant in range(4):
             nc.sync.dma_start(
                 out=w_scales[32 * quadrant : 32 * quadrant + 4].bitcast(I32),
@@ -187,7 +176,7 @@ def tile_occurrencepool_pa_kernel(
 
         def turned_bank(i, tile):
             c0 = tile * P
-            chan_ps = psum_chan.tile([P, K_PASS], F32, name="chan_ps")
+            chan_ps = psum_chan.tile([P, K_PASS], F32, tag="chan")
             for g in range(K_PASSES):
                 nc.tensor.matmul_mx(
                     out=chan_ps[:],
@@ -289,28 +278,30 @@ def tile_occurrencepool_pa_kernel(
 
         bias_all = consts.tile([P, CIN], F32)
         turned_bias = consts.tile([P, len(TURNED)], F32)
-        for g in range(K_PASSES):
-            share = 3 * P
-            regroup(0, g, 0, share, "vector")
-            regroup(0, g, share, K_PASS, "scalar")
-            quantise_h(0, g)
-            keep_busy(h_grp[0][:, g, 0:P, :].rearrange("p v t -> p (v t)"), 3)
-            cols = slice(g * BANK, (g + 1) * BANK)
+        def spread_bias(half):
+            cols = slice(half * BANK, (half + 1) * BANK)
             bias_ps = psum_misc.tile([P, BANK], F32, tag="misc")
             nc.tensor.matmul(bias_ps[:], lhsT=ones[:], rhs=bias_row[:, cols], start=True, stop=True)
             nc.scalar.copy(out=bias_all[:, cols], in_=bias_ps[:])
 
-        def head_extras():
-            turned_bias_ps = psum_misc.tile([P, len(TURNED)], F32, tag="misc")
-            for k, tile in enumerate(TURNED):
-                nc.tensor.matmul(
-                    turned_bias_ps[:, k : k + 1],
-                    lhsT=bias_row[:, tile * P : (tile + 1) * P],
-                    rhs=ones[:, 0:1],
-                    start=True,
-                    stop=True,
-                )
-            nc.scalar.copy(out=turned_bias[:], in_=turned_bias_ps[:])
+        turned_bias_ps = psum_chan.tile([P, len(TURNED)], F32, tag="chan")
+        for k, tile in enumerate(TURNED):
+            nc.tensor.matmul(
+                turned_bias_ps[:, k : k + 1],
+                lhsT=bias_row[:, tile * P : (tile + 1) * P],
+                rhs=ones[:, 0:1],
+                start=True,
+                stop=True,
+            )
+        nc.scalar.copy(out=turned_bias[:], in_=turned_bias_ps[:])
+        spread_bias(0)
+        for g, share in enumerate((5 * P // 2, 2 * P)):
+            regroup(0, g, 0, share, "vector")
+            regroup(0, g, share, K_PASS, "scalar")
+            quantise_h(0, g)
+        spread_bias(1)
+
+        def turn_weight():
             w_occT_ps = psum_misc.tile([C8, COUT], BF16, tag="misc")
             nc.tensor.transpose(w_occT_ps[:], w_occ_sb[:], identity[:])
             nc.scalar.copy(out=w_occT[:], in_=w_occT_ps[:])
@@ -327,7 +318,7 @@ def tile_occurrencepool_pa_kernel(
                     if tile < PIECES:
                         regroup_piece(PIECES + tile)
                     if tile == 4:
-                        head_extras()
+                        turn_weight()
                         quantise_f(i, 0, 0, BANK)
                     if tile == 5:
                         occurrence(0)

@@ -35,7 +35,7 @@ WORDS = PACK // 2
 TILES = CIN // P
 PIECE = K_PASS // 2
 PIECES = K_PASSES * 2
-TURNED = (0, BANKS_PER_HALF)
+TURNED = (TILES - 2, TILES - 1)
 
 FLOPS = 2 * B * S * (CIN * CMID + COUT * C8 + COUT * CIN)
 
@@ -73,6 +73,8 @@ def tile_occurrencepool_pa_kernel(
         nc.gpsimd.memset(ones[:], 1.0)
         warm = consts.tile([P, 1], F32)
         nc.scalar.activation(out=warm[:], in_=ones[:, 0:1], func=ACT.Abs)
+        busy = consts.tile([P, BANK], BF16)
+        nc.gpsimd.memset(busy[:], 0.0)
         identity = consts.tile([P, P], BF16)
         masks.make_identity(nc, identity[:])
         identity_f32 = consts.tile([P, P], F32)
@@ -86,20 +88,30 @@ def tile_occurrencepool_pa_kernel(
                 .rearrange("g r n -> r g n")
                 .bitcast(I32),
             )
-        w_words = consts.tile([P, K_PASSES, 2 * CIN], U8, align_bytes=64)
+        w_words = []
         for half in range(HALVES):
+            words = consts.tile([P, K_PASSES, 2 * BANK], U8, name="w_words_%d" % half, align_bytes=64)
+            w_words.append(words)
             cols = slice(half * 2 * BANK, (half + 1) * 2 * BANK)
             nc.sync.dma_start(
-                out=w_words[:, :, cols].bitcast(I32),
+                out=words[:].bitcast(I32),
                 in_=w_add2_words[:, :, cols].rearrange("g p n -> p g n").bitcast(I32),
             )
-        h_raw.append(load_h(1))
+            if half == 0:
+                h_raw.append(load_h(1))
         w_occ_sb = consts.tile([COUT, C8], BF16)
         nc.sync.dma_start(out=w_occ_sb[:], in_=w_occ3)
         h_occ_sb = consts.tile([C8, B, S], BF16)
         nc.sync.dma_start(out=h_occ_sb[:], in_=h_occ.rearrange("b c v -> c b v"))
         h_raw.append(load_h(2))
         h_raw.append(load_h(3))
+
+        def weight(g, c0):
+            half, c = divmod(c0, BANK)
+            return (
+                w_words[half][:, g, 2 * c : 2 * (c + P)].bitcast(FP4X4),
+                w_scales[:, g, c0 : c0 + P],
+            )
 
         h_grp = []
         h_codes = []
@@ -117,6 +129,10 @@ def tile_occurrencepool_pa_kernel(
             src = h_raw[i][:, g, :, v0:v1].rearrange("p t v -> p v t")
             if engine == "vector":
                 nc.vector.tensor_copy(out=dst, in_=src)
+            elif engine == "gpsimd":
+                nc.gpsimd.tensor_scalar(
+                    out=dst, in0=src, scalar1=1.0, scalar2=0.0, op0=ALU.mult, op1=ALU.add
+                )
             else:
                 nc.scalar.copy(out=dst, in_=src)
 
@@ -124,9 +140,12 @@ def tile_occurrencepool_pa_kernel(
             i, q = divmod(r, PIECES)
             if i < N_CHUNKS:
                 g, part = divmod(q, 2)
-                regroup(
-                    i, g, part * PIECE, (part + 1) * PIECE, "vector" if q == 0 else "scalar"
-                )
+                v0 = part * PIECE
+                if q == 0:
+                    for v in range(v0, v0 + PIECE, PIECE // 4):
+                        regroup(i, g, v, v + PIECE // 4, "gpsimd")
+                else:
+                    regroup(i, g, v0, v0 + PIECE, "scalar")
 
         def quantise_h(i, g):
             if i < N_CHUNKS:
@@ -158,12 +177,13 @@ def tile_occurrencepool_pa_kernel(
             for t in range(PACK):
                 voxels = slice(t * P, (t + 1) * P)
                 for g in range(K_PASSES):
+                    w, w_scale = weight(g, c0)
                     nc.tensor.matmul_mx(
                         out=feat_ps[:, t, :],
                         lhsT=h_codes[i][:, g, voxels].bitcast(FP8X4),
                         lhsT_scale=h_scales[i][:, g, voxels],
-                        rhs=w_words[:, g, 2 * c0 : 2 * (c0 + P)].bitcast(FP4X4),
-                        rhs_scale=w_scales[:, g, c0 : c0 + P],
+                        rhs=w,
+                        rhs_scale=w_scale,
                         start=(g == 0),
                         stop=(g == K_PASSES - 1),
                     )
@@ -178,10 +198,11 @@ def tile_occurrencepool_pa_kernel(
             c0 = tile * P
             chan_ps = psum_chan.tile([P, K_PASS], F32, tag="chan")
             for g in range(K_PASSES):
+                w, w_scale = weight(g, c0)
                 nc.tensor.matmul_mx(
                     out=chan_ps[:],
-                    lhsT=w_words[:, g, 2 * c0 : 2 * (c0 + P)].bitcast(FP4X4),
-                    lhsT_scale=w_scales[:, g, c0 : c0 + P],
+                    lhsT=w,
+                    lhsT_scale=w_scale,
                     rhs=h_codes[i][:, g, :].bitcast(FP8X4),
                     rhs_scale=h_scales[i][:, g, :],
                     start=(g == 0),
@@ -205,11 +226,13 @@ def tile_occurrencepool_pa_kernel(
                     nc.tensor.transpose(
                         turned_ps[:, k, u, :], words[:, u * P : (u + 1) * P], identity_f32[:]
                     )
-            for k, tile in enumerate(TURNED):
-                nc.scalar.copy(
-                    out=tile_cols(i, tile).rearrange("p c t -> p (c t)").bitcast(F32),
-                    in_=turned_ps[:, k].rearrange("p u c -> p c u"),
-                )
+            cols = slice((TURNED[0] - BANKS_PER_HALF) * P, BANK)
+            nc.scalar.copy(
+                out=f_grp[i, 1][:, cols, :]
+                .bitcast(F32)
+                .rearrange("p (k c) u -> p k c u", k=len(TURNED)),
+                in_=turned_ps[:].rearrange("p k u c -> p k c u"),
+            )
 
         def quantise_f(i, half, c0, c1):
             nc.vector.quantize_mx(
@@ -247,7 +270,7 @@ def tile_occurrencepool_pa_kernel(
             )
 
         def pool_half(b, half, c0, c1, engine):
-            acc = psum_misc.tile([COUT, BANK], F32, tag="misc")
+            acc = psum_chan.tile([COUT, BANK], F32, tag="chan")
             for vg in range(V_PASSES):
                 i = b * V_PASSES + vg
                 nc.tensor.matmul_mx(
@@ -284,6 +307,12 @@ def tile_occurrencepool_pa_kernel(
             nc.tensor.matmul(bias_ps[:], lhsT=ones[:], rhs=bias_row[:, cols], start=True, stop=True)
             nc.scalar.copy(out=bias_all[:, cols], in_=bias_ps[:])
 
+        def keep_busy(rhs, count):
+            idle_ps = psum_misc.tile([P, BANK], F32, tag="misc")
+            for k in range(count):
+                nc.tensor.matmul(idle_ps[:], lhsT=ones[:], rhs=rhs, start=True, stop=True)
+
+        keep_busy(busy[:], 6)
         turned_bias_ps = psum_chan.tile([P, len(TURNED)], F32, tag="chan")
         for k, tile in enumerate(TURNED):
             nc.tensor.matmul(
@@ -312,53 +341,43 @@ def tile_occurrencepool_pa_kernel(
             b, vg = divmod(i, V_PASSES)
             for half in range(HALVES):
                 open_half(i, half)
-            if i == 0:
-                for tile in range(TILES):
-                    feature_bank(i, tile)
-                    if tile < PIECES:
-                        regroup_piece(PIECES + tile)
-                    if tile == 4:
-                        turn_weight()
-                        quantise_f(i, 0, 0, BANK)
-                    if tile == 5:
-                        occurrence(0)
-                        occurrence(1)
-                        quantise_h(1, 0)
-                    if tile == 6:
-                        quantise_h(1, 1)
-                        regroup_piece(2 * PIECES)
-                continue
-            chans = [turned_bank(i, TURNED[0])]
-            regroup_piece((i + 1) * PIECES + 1)
+            last = i == N_CHUNKS - 1
+            if i == 1:
+                turn_weight()
+            feature_bank(i, 0)
+            if i > 0:
+                chans = [turned_bank(i, tile) for tile in TURNED]
             feature_bank(i, 1)
-            quantise_f(i - 1, 1, 0, BANK)
-            chans.append(turned_bank(i, TURNED[1]))
-            regroup_piece((i + 1) * PIECES + 2)
-            feature_bank(i, 2)
-            if i == 1:
-                quantise_occ(0)
-            if i == 2:
-                quantise_occ(1)
+            if i > 0:
+                quantise_f(i - 1, 1, 0, BANK)
+            for q in range(PIECES):
+                regroup_piece((i + 1) * PIECES + q)
             quantise_h(i + 1, 0)
-            feature_bank(i, 3)
-            turn(i, chans)
-            regroup_piece((i + 1) * PIECES + 3)
-            feature_bank(i, 5)
+            feature_bank(i, 2)
             quantise_h(i + 1, 1)
-            if i == 2:
-                pool_half(0, 1, 0, BANK, "scalar")
+            feature_bank(i, 3)
+            if i == 0:
+                chans = [turned_bank(i, tile) for tile in TURNED]
+            if last:
+                turn(i, chans)
+            feature_bank(i, 4)
             quantise_f(i, 0, 0, BANK)
-            feature_bank(i, 6)
-            regroup_piece((i + 2) * PIECES)
-            if i == 1:
-                occurrence(2)
-                occurrence(3)
-            if i == N_CHUNKS - 1:
-                quantise_f(i, 1, 0, 2 * P)
-            feature_bank(i, 7)
-            if vg == V_PASSES - 1:
+            if last:
+                quantise_f(i, 1, 2 * P, BANK)
+            feature_bank(i, 5)
+            if not last:
+                turn(i, chans)
+            if i in (1, 2):
+                b_occ = i - 1
+                occurrence(b_occ * V_PASSES)
+                occurrence(b_occ * V_PASSES + 1)
+                quantise_occ(b_occ)
+            if i == 2:
+                pool_half(0, 0, 0, BANK, "scalar")
+                pool_half(0, 1, 0, BANK, "scalar")
+            if last:
                 pool_half(b, 0, 0, BANK, "scalar")
         i = N_CHUNKS - 1
-        pool_half(B - 1, 1, 0, 2 * P, "scalar")
-        quantise_f(i, 1, 2 * P, BANK)
-        pool_half(B - 1, 1, 2 * P, BANK, "vector")
+        pool_half(B - 1, 1, 2 * P, BANK, "scalar")
+        quantise_f(i, 1, 0, 2 * P)
+        pool_half(B - 1, 1, 0, 2 * P, "vector")

@@ -125,8 +125,8 @@ def tile_occurrencepool_pa_kernel(
             h_scales.append(scales)
 
         def regroup(i, g, v0, v1, engine):
-            dst = h_grp[i][:, g, v0:v1, :]
-            src = h_raw[i][:, g, :, v0:v1].rearrange("p t v -> p v t")
+            dst = h_grp[i][:, g, v0:v1, :].rearrange("p (c i) t -> p c t i", i=PACK)
+            src = h_raw[i][:, g, :, v0:v1].rearrange("p t (c i) -> p c t i", i=PACK)
             if engine == "vector":
                 nc.vector.tensor_copy(out=dst, in_=src)
             elif engine == "gpsimd":
@@ -324,10 +324,12 @@ def tile_occurrencepool_pa_kernel(
             )
         nc.scalar.copy(out=turned_bias[:], in_=turned_bias_ps[:])
         spread_bias(0)
-        for g, share in enumerate((5 * P // 2, 2 * P)):
-            regroup(0, g, 0, share, "vector")
-            regroup(0, g, share, K_PASS, "scalar")
-            quantise_h(0, g)
+        with tc.manual_schedule(engines={mybir.EngineType.DVE}):
+            for g, share in enumerate((11 * P // 4, 5 * P // 2)):
+                regroup(0, g, 0, share, "vector")
+                regroup(0, g, share, K_PASS, "scalar")
+            for g in range(K_PASSES):
+                quantise_h(0, g)
         spread_bias(1)
 
         def turn_weight():
@@ -345,9 +347,9 @@ def tile_occurrencepool_pa_kernel(
             if i == 1:
                 turn_weight()
             feature_bank(i, 0)
+            feature_bank(i, 1)
             if i > 0:
                 chans = [turned_bank(i, tile) for tile in TURNED]
-            feature_bank(i, 1)
             if i > 0:
                 quantise_f(i - 1, 1, 0, BANK)
             for q in range(PIECES):
@@ -364,6 +366,7 @@ def tile_occurrencepool_pa_kernel(
             quantise_f(i, 0, 0, BANK)
             if last:
                 quantise_f(i, 1, 2 * P, BANK)
+                quantise_f(i, 1, 0, P)
             feature_bank(i, 5)
             if not last:
                 turn(i, chans)
@@ -379,5 +382,6 @@ def tile_occurrencepool_pa_kernel(
                 pool_half(b, 0, 0, BANK, "scalar")
         i = N_CHUNKS - 1
         pool_half(B - 1, 1, 2 * P, BANK, "scalar")
-        quantise_f(i, 1, 0, 2 * P)
-        pool_half(B - 1, 1, 0, 2 * P, "vector")
+        pool_half(B - 1, 1, 0, P, "scalar")
+        quantise_f(i, 1, P, 2 * P)
+        pool_half(B - 1, 1, P, 2 * P, "vector")

from contextlib import ExitStack

import concourse.masks as masks
import concourse.mybir as mybir

F32 = mybir.dt.float32
BF16 = mybir.dt.bfloat16
I32 = mybir.dt.int32
U32 = mybir.dt.uint32
U8 = mybir.dt.uint8
FP8X4 = mybir.dt.float8_e4m3fn_x4
FP4X4 = mybir.dt.float4_e2m1fn_x4
ACT = mybir.ActivationFunctionType
ALU = mybir.AluOpType

P = 128
PACK = 4
K_PASS = P * PACK
BANK = 512

B = 2
CMID = 1024
CIN = 1024
C8 = 128
COUT = 128
S = 1024

K_PASSES = CMID // K_PASS
V_PASSES = S // K_PASS
N_CHUNKS = B * V_PASSES
HALVES = CIN // BANK
BANKS_PER_HALF = BANK // P

WORDS = PACK // 2
TILES = CIN // P
PIECE = K_PASS // 2
PIECES = K_PASSES * 2
TURNED = (TILES - 2, TILES - 1)

FLOPS = 2 * B * S * (CIN * CMID + COUT * C8 + COUT * CIN)


def tile_occurrencepool_pa_kernel(
    tc, h_add, w_add2_words, w_add2_scales, b_add2, h_occ, w_occ3, out
):
    nc = tc.nc
    with ExitStack() as ctx:
        consts = ctx.enter_context(tc.tile_pool(name="consts", bufs=1))
        raws = ctx.enter_context(tc.tile_pool(name="raws", bufs=N_CHUNKS))
        work = ctx.enter_context(tc.tile_pool(name="work", bufs=4))
        psum_feat = ctx.enter_context(tc.psum_pool(name="psum_feat", bufs=4))
        psum_chan = ctx.enter_context(tc.psum_pool(name="psum_chan", bufs=2))
        psum_misc = ctx.enter_context(tc.psum_pool(name="psum_misc", bufs=2))

        def load_h(i):
            b, vg = divmod(i, V_PASSES)
            raw = raws.tile([P, K_PASSES, PACK, K_PASS], BF16, name="h_raw")
            for g in range(K_PASSES):
                nc.sync.dma_start(
                    out=raw[:, g],
                    in_=h_add[
                        b, g * K_PASS : (g + 1) * K_PASS, vg * K_PASS : (vg + 1) * K_PASS
                    ].rearrange("(p t) v -> p t v", t=PACK),
                )
            return raw

        bias_row = consts.tile([P, CIN], BF16)
        nc.vector.memset(bias_row[:].bitcast(I32), 0)
        nc.scalar.dma_start(out=bias_row[0:1, :], in_=b_add2.rearrange("(o c) -> o c", o=1))
        w_scales = consts.tile([P, K_PASSES, CIN], U8, align_bytes=64)
        nc.vector.memset(w_scales[:].bitcast(I32), 0)
        ones = consts.tile([P, P], BF16)
        nc.gpsimd.memset(ones[:], 1.0)
        warm = consts.tile([P, 1], F32)
        nc.scalar.activation(out=warm[:], in_=ones[:, 0:1], func=ACT.Abs)
        busy = consts.tile([P, BANK], BF16)
        nc.gpsimd.memset(busy[:], 0.0)
        identity = consts.tile([P, P], BF16)
        masks.make_identity(nc, identity[:])
        identity_f32 = consts.tile([P, P], F32)
        masks.make_identity(nc, identity_f32[:])

        h_raw = [load_h(0)]
        for quadrant in range(4):
            nc.sync.dma_start(
                out=w_scales[32 * quadrant : 32 * quadrant + 4].bitcast(I32),
                in_=w_add2_scales[:, 4 * quadrant : 4 * quadrant + 4, :]
                .rearrange("g r n -> r g n")
                .bitcast(I32),
            )
        w_words = []
        for half in range(HALVES):
            words = consts.tile([P, K_PASSES, 2 * BANK], U8, name="w_words_%d" % half, align_bytes=64)
            w_words.append(words)
            cols = slice(half * 2 * BANK, (half + 1) * 2 * BANK)
            nc.sync.dma_start(
                out=words[:].bitcast(I32),
                in_=w_add2_words[:, :, cols].rearrange("g p n -> p g n").bitcast(I32),
            )
            if half == 0:
                h_raw.append(load_h(1))
        w_occ_sb = consts.tile([COUT, C8], BF16)
        nc.sync.dma_start(out=w_occ_sb[:], in_=w_occ3)
        h_occ_sb = consts.tile([C8, B, S], BF16)
        nc.sync.dma_start(out=h_occ_sb[:], in_=h_occ.rearrange("b c v -> c b v"))
        h_raw.append(load_h(2))
        h_raw.append(load_h(3))

        def weight(g, c0):
            half, c = divmod(c0, BANK)
            return (
                w_words[half][:, g, 2 * c : 2 * (c + P)].bitcast(FP4X4),
                w_scales[:, g, c0 : c0 + P],
            )

        h_grp = []
        h_codes = []
        h_scales = []
        for i in range(N_CHUNKS):
            grp = work.tile([P, K_PASSES, K_PASS, PACK], BF16, name="h_grp", align_bytes=64)
            codes = work.tile([P, K_PASSES, K_PASS], U32, name="h_codes", align_bytes=64)
            scales = work.tile([P, K_PASSES, K_PASS], U8, name="h_scales", align_bytes=64)
            h_grp.append(grp)
            h_codes.append(codes)
            h_scales.append(scales)

        def regroup(i, g, v0, v1, engine):
            dst = h_grp[i][:, g, v0:v1, :].rearrange("p (c i) t -> p c t i", i=PACK)
            src = h_raw[i][:, g, :, v0:v1].rearrange("p t (c i) -> p c t i", i=PACK)
            if engine == "vector":
                nc.vector.tensor_copy(out=dst, in_=src)
            elif engine == "gpsimd":
                nc.gpsimd.tensor_scalar(
                    out=dst, in0=src, scalar1=1.0, scalar2=0.0, op0=ALU.mult, op1=ALU.add
                )
            else:
                nc.scalar.copy(out=dst, in_=src)

        def regroup_piece(r):
            i, q = divmod(r, PIECES)
            if i < N_CHUNKS:
                g, part = divmod(q, 2)
                v0 = part * PIECE
                if q == 0:
                    for v in range(v0, v0 + PIECE, PIECE // 4):
                        regroup(i, g, v, v + PIECE // 4, "gpsimd")
                else:
                    regroup(i, g, v0, v0 + PIECE, "scalar")

        def quantise_h(i, g):
            if i < N_CHUNKS:
                nc.vector.quantize_mx(
                    out=h_codes[i][:, g].bitcast(FP8X4),
                    scales=h_scales[i][:, g],
                    in_=h_grp[i][:, g].rearrange("p v t -> p (v t)"),
                )

        f_grp = {}
        f_codes = {}
        f_scales = {}

        def open_half(i, half):
            grp = work.tile([P, BANK, PACK], BF16, name="f_grp", align_bytes=64)
            codes = work.tile([P, BANK], U32, name="f_codes", align_bytes=64)
            scales = work.tile([P, BANK], U8, name="f_scales", align_bytes=64)
            f_grp[i, half] = grp
            f_codes[i, half] = codes
            f_scales[i, half] = scales

        def tile_cols(i, tile):
            half, j = divmod(tile, BANKS_PER_HALF)
            return f_grp[i, half][:, j * P : (j + 1) * P, :]

        def feature_bank(i, tile):
            c0 = tile * P
            feat_ps = psum_feat.tile([P, PACK, P], F32, name="feat_ps")
            for t in range(PACK):
                voxels = slice(t * P, (t + 1) * P)
                for g in range(K_PASSES):
                    w, w_scale = weight(g, c0)
                    nc.tensor.matmul_mx(
                        out=feat_ps[:, t, :],
                        lhsT=h_codes[i][:, g, voxels].bitcast(FP8X4),
                        lhsT_scale=h_scales[i][:, g, voxels],
                        rhs=w,
                        rhs_scale=w_scale,
                        start=(g == 0),
                        stop=(g == K_PASSES - 1),
                    )
            nc.vector.tensor_tensor(
                out=tile_cols(i, tile),
                in0=feat_ps[:].rearrange("p t c -> p c t"),
                in1=bias_all[:, c0 : c0 + P].unsqueeze(2).to_broadcast([P, P, PACK]),
                op=ALU.add,
            )

        def turned_bank(i, tile):
            c0 = tile * P
            chan_ps = psum_chan.tile([P, K_PASS], F32, tag="chan")
            for g in range(K_PASSES):
                w, w_scale = weight(g, c0)
                nc.tensor.matmul_mx(
                    out=chan_ps[:],
                    lhsT=w,
                    lhsT_scale=w_scale,
                    rhs=h_codes[i][:, g, :].bitcast(FP8X4),
                    rhs_scale=h_scales[i][:, g, :],
                    start=(g == 0),
                    stop=(g == K_PASSES - 1),
                )
            chan = work.tile([P, WORDS, P, 2], BF16, name="chan", align_bytes=64)
            k = TURNED.index(tile)
            nc.scalar.activation(
                out=chan[:],
                in_=chan_ps[:].rearrange("c (u e p) -> c u p e", u=WORDS, e=2),
                func=ACT.Identity,
                bias=turned_bias[:, k : k + 1],
            )
            return chan

        def turn(i, chans):
            turned_ps = psum_misc.tile([P, len(TURNED), WORDS, P], F32, tag="misc")
            for k, chan in enumerate(chans):
                words = chan[:].rearrange("c u p e -> c (u p e)").bitcast(F32)
                for u in range(WORDS):
                    nc.tensor.transpose(
                        turned_ps[:, k, u, :], words[:, u * P : (u + 1) * P], identity_f32[:]
                    )
            cols = slice((TURNED[0] - BANKS_PER_HALF) * P, BANK)
            nc.scalar.copy(
                out=f_grp[i, 1][:, cols, :]
                .bitcast(F32)
                .rearrange("p (k c) u -> p k c u", k=len(TURNED)),
                in_=turned_ps[:].rearrange("p k u c -> p k c u"),
            )

        def quantise_f(i, half, c0, c1):
            nc.vector.quantize_mx(
                out=f_codes[i, half][:, c0:c1].bitcast(FP8X4),
                scales=f_scales[i, half][:, c0:c1],
                in_=f_grp[i, half][:, c0:c1].rearrange("p c t -> p (c t)"),
            )

        occ_grp = consts.tile([P, N_CHUNKS, COUT, PACK], BF16, align_bytes=64)
        occ_codes = consts.tile([P, N_CHUNKS, COUT], U32, align_bytes=64)
        occ_scales = consts.tile([P, N_CHUNKS, COUT], U8, align_bytes=64)

        def occurrence(i):
            b, vg = divmod(i, V_PASSES)
            occ_ps = psum_misc.tile([P, PACK, COUT], F32, tag="misc")
            for t in range(PACK):
                v0 = vg * K_PASS + t * P
                nc.tensor.matmul(
                    occ_ps[:, t, :],
                    lhsT=h_occ_sb[:, b, v0 : v0 + P],
                    rhs=w_occT[:],
                    start=True,
                    stop=True,
                )
            nc.scalar.activation(
                out=occ_grp[:, i], in_=occ_ps[:].rearrange("p t o -> p o t"), func=ACT.Abs
            )

        def quantise_occ(b):
            sample = slice(b * V_PASSES, (b + 1) * V_PASSES)
            nc.vector.quantize_mx(
                out=occ_codes[:, sample].rearrange("p i o -> p (i o)").bitcast(FP8X4),
                scales=occ_scales[:, sample].rearrange("p i o -> p (i o)"),
                in_=occ_grp[:, sample].rearrange("p i o t -> p (i o t)"),
            )

        def pool_half(b, half, c0, c1, engine):
            acc = psum_chan.tile([COUT, BANK], F32, tag="chan")
            for vg in range(V_PASSES):
                i = b * V_PASSES + vg
                nc.tensor.matmul_mx(
                    out=acc[:, : c1 - c0],
                    lhsT=occ_codes[:, i, :].bitcast(FP8X4),
                    lhsT_scale=occ_scales[:, i, :],
                    rhs=f_codes[i, half][:, c0:c1].bitcast(FP8X4),
                    rhs_scale=f_scales[i, half][:, c0:c1],
                    start=(vg == 0),
                    stop=(vg == V_PASSES - 1),
                )
            out_sb = work.tile([COUT, BANK], F32, name="out_sb")
            if engine == "vector":
                nc.vector.tensor_scalar(
                    out=out_sb[:, : c1 - c0],
                    in0=acc[:, : c1 - c0],
                    scalar1=1.0 / S,
                    scalar2=None,
                    op0=ALU.mult,
                )
            else:
                nc.scalar.activation(
                    out=out_sb[:, : c1 - c0], in_=acc[:, : c1 - c0], func=ACT.Copy, scale=1.0 / S
                )
            nc.sync.dma_start(
                out=out[b, :, half * BANK + c0 : half * BANK + c1], in_=out_sb[:, : c1 - c0]
            )

        bias_all = consts.tile([P, CIN], F32)
        turned_bias = consts.tile([P, len(TURNED)], F32)
        def spread_bias(half):
            cols = slice(half * BANK, (half + 1) * BANK)
            bias_ps = psum_misc.tile([P, BANK], F32, tag="misc")
            nc.tensor.matmul(bias_ps[:], lhsT=ones[:], rhs=bias_row[:, cols], start=True, stop=True)
            nc.scalar.copy(out=bias_all[:, cols], in_=bias_ps[:])

        def keep_busy(rhs, count):
            idle_ps = psum_misc.tile([P, BANK], F32, tag="misc")
            for k in range(count):
                nc.tensor.matmul(idle_ps[:], lhsT=ones[:], rhs=rhs, start=True, stop=True)

        keep_busy(busy[:], 6)
        turned_bias_ps = psum_chan.tile([P, len(TURNED)], F32, tag="chan")
        for k, tile in enumerate(TURNED):
            nc.tensor.matmul(
                turned_bias_ps[:, k : k + 1],
                lhsT=bias_row[:, tile * P : (tile + 1) * P],
                rhs=ones[:, 0:1],
                start=True,
                stop=True,
            )
        nc.scalar.copy(out=turned_bias[:], in_=turned_bias_ps[:])
        spread_bias(0)
        with tc.manual_schedule(engines={mybir.EngineType.DVE}):
            for g, share in enumerate((11 * P // 4, 5 * P // 2)):
                regroup(0, g, 0, share, "vector")
                regroup(0, g, share, K_PASS, "scalar")
            for g in range(K_PASSES):
                quantise_h(0, g)
        spread_bias(1)

        def turn_weight():
            w_occT_ps = psum_misc.tile([C8, COUT], BF16, tag="misc")
            nc.tensor.transpose(w_occT_ps[:], w_occ_sb[:], identity[:])
            nc.scalar.copy(out=w_occT[:], in_=w_occT_ps[:])

        w_occT = consts.tile([C8, COUT], BF16)

        for i in range(N_CHUNKS):
            b, vg = divmod(i, V_PASSES)
            for half in range(HALVES):
                open_half(i, half)
            last = i == N_CHUNKS - 1
            if i == 1:
                turn_weight()
            feature_bank(i, 0)
            feature_bank(i, 1)
            if i > 0:
                chans = [turned_bank(i, tile) for tile in TURNED]
            if i > 0:
                quantise_f(i - 1, 1, 0, BANK)
            for q in range(PIECES):
                regroup_piece((i + 1) * PIECES + q)
            quantise_h(i + 1, 0)
            feature_bank(i, 2)
            quantise_h(i + 1, 1)
            feature_bank(i, 3)
            if i == 0:
                chans = [turned_bank(i, tile) for tile in TURNED]
            if last:
                turn(i, chans)
            feature_bank(i, 4)
            quantise_f(i, 0, 0, BANK)
            if last:
                quantise_f(i, 1, 2 * P, BANK)
                quantise_f(i, 1, 0, P)
            feature_bank(i, 5)
            if not last:
                turn(i, chans)
            if i in (1, 2):
                b_occ = i - 1
                occurrence(b_occ * V_PASSES)
                occurrence(b_occ * V_PASSES + 1)
                quantise_occ(b_occ)
            if i == 2:
                pool_half(0, 0, 0, BANK, "scalar")
                pool_half(0, 1, 0, BANK, "scalar")
            if last:
                pool_half(b, 0, 0, BANK, "scalar")
        i = N_CHUNKS - 1
        pool_half(B - 1, 1, 2 * P, BANK, "scalar")
        pool_half(B - 1, 1, 0, P, "scalar")
        quantise_f(i, 1, P, 2 * P)
        pool_half(B - 1, 1, P, 2 * P, "vector")
